import numpy as np
import ml_dtypes


def mxq(x, axis, fmt="e4m3"):
    dtype, down = {"e4m3": (ml_dtypes.float8_e4m3fn, 7), "e5m2": (ml_dtypes.float8_e5m2, 14)}[fmt]
    v = np.moveaxis(np.asarray(x, np.float32).astype(ml_dtypes.bfloat16).astype(np.float64), axis, -1)
    blocks = v.reshape(v.shape[:-1] + (-1, 32))
    amax = np.abs(blocks).max(-1, keepdims=True)
    byte = np.maximum(np.where(amax > 0, np.frexp(amax)[1] - 1 + 127, 0) - down, 1)
    scale = np.exp2(byte - 127.0)
    codes = (blocks / scale).astype(np.float32).astype(dtype).astype(np.float64)
    return np.moveaxis((codes * scale).reshape(v.shape), -1, axis)


WIDE = False


def mx_kscale(k):
    if not WIDE:
        return np.ones(k)
    levels = np.array([18, -18])
    if k % 512:
        return np.exp2(np.random.permutation(np.resize(levels, k // 32))).repeat(32)
    a = np.empty((k // 512, 16))
    for p in range(k // 512):
        a[p, :8] = np.random.permutation(np.resize(levels, 8))
        for g in range(8):
            far = levels[np.abs(levels - a[p, g]) >= 10]
            a[p, g + 8] = far[np.random.randint(len(far))]
    return np.exp2(a.ravel()).repeat(32)


BF16 = ml_dtypes.bfloat16


def bf(x):
    return np.asarray(x, np.float32).astype(BF16)


def f64(x):
    return np.asarray(x).astype(np.float64)


B, I, C, S2 = 4, 32, 512, 8
P = S2 * S2
T = B * I * P


def setup_inputs():
    s = mx_kscale(T).reshape(B, I, P)[:, :, 0]
    u = mx_kscale(C)
    q = bf(np.random.standard_normal((B, I, C)) * s[:, :, None])
    feats = bf(np.random.standard_normal((B, C, S2, S2)))
    po_w = bf(np.random.standard_normal((C, C)) / np.sqrt(C) / u[:, None])
    po_b = bf(np.random.standard_normal(C) * 0.3)
    g = np.random.standard_normal((B, I, C, S2, S2)) * np.exp2(np.random.randint(-6, 1, (B, I, 1, S2, S2))) * 0.5
    grad_out = bf(g / s[:, :, None, None, None] * u[:, None, None])
    return {"q": q, "feats": feats, "po_w": po_w, "po_b": po_b, "grad_out": grad_out}


def reference(q, feats, po_w, po_b, grad_out):
    qf = f64(q)
    m = qf[:, :, :, None] * f64(feats).reshape(B, 1, C, P)
    mt = m.transpose(2, 0, 1, 3).reshape(C, T)
    g = f64(grad_out).reshape(B, I, C, P).transpose(2, 0, 1, 3).reshape(C, T)
    dm = mxq(f64(po_w), 0, "e4m3").T @ mxq(g, 0, "e5m2")
    qt = qf.transpose(2, 0, 1)[:, :, :, None]
    dfeats = (dm.reshape(C, B, I, P) * qt).sum(axis=2)
    dfeats = dfeats.transpose(1, 0, 2).reshape(B, C, S2, S2)
    dw = mxq(g, 1, "e5m2") @ mxq(mt, 1, "e4m3").T
    return dfeats, dw

@@ -1,0 +1,294 @@
+from contextlib import ExitStack
+
+import concourse.mybir as mybir
+from concourse.masks import make_identity
+
+B, I, C, P64 = 4, 32, 512, 64
+PASSES = 16
+FLOPS = 2 * 2 * 8192 * 512 * 512
+BYTES = 2 * (4 * 32 * 512 + 4 * 512 * 64 + 512 * 512 + 4 * 32 * 512 * 64) + 4 * (4 * 512 * 64 + 512 * 512)
+
+F32 = mybir.dt.float32
+BF16 = mybir.dt.bfloat16
+U32 = mybir.dt.uint32
+U8 = mybir.dt.uint8
+E4M3 = mybir.dt.float8_e4m3fn_x4
+E5M2 = mybir.dt.float8_e5m2_x4
+ADD = mybir.AluOpType.add
+MULT = mybir.AluOpType.mult
+P = 128
+
+
+def tile_rpn_modulator_pb_v_kernel(tc, q, feats, po_w, po_b, grad_out, out_0, out_1):
+    nc = tc.nc
+    with ExitStack() as ctx:
+        keep = ctx.enter_context(tc.tile_pool(name="keep", bufs=1))
+        work = ctx.enter_context(tc.tile_pool(name="work", bufs=2))
+        psum = ctx.enter_context(tc.psum_pool(name="psum", bufs=1))
+        ctx.enter_context(tc.manual_schedule())
+
+        raws = {}
+
+        def load(g, pieces=1):
+            t = work.tile([P, 8, 4, P64], BF16, name="raw", tag="raw", bufs=8, align_bytes=64)
+            b, i0 = g // 4, 8 * (g % 4)
+            n = 8 // pieces
+            for k in range(pieces):
+                nc.sync.dma_start(
+                    out=t[:, k * n:(k + 1) * n].rearrange("q i j w -> q i (j w)"),
+                    in_=grad_out[b, i0 + k * n:i0 + (k + 1) * n].rearrange("i (q j) y x -> q i (j y x)", j=4))
+            raws[g] = t
+
+        load(0, 4)
+        w_raw = keep.tile([P, 4, C], BF16, name="w_raw", align_bytes=64)
+        nc.sync.dma_start(out=w_raw[:], in_=po_w.rearrange("(q j) c -> q j c", j=4))
+        q_sb = keep.tile([P, C], BF16, name="q_sb", align_bytes=64)
+        nc.sync.dma_start(out=q_sb[:], in_=q.rearrange("b i c -> (b i) c"))
+        load(1)
+        f_sb = keep.tile([P, 16, P64], BF16, name="f_sb", align_bytes=64)
+        nc.sync.dma_start(out=f_sb[:], in_=feats.rearrange("b (k r) y x -> r (b k) (y x)", r=P))
+        for g in range(2, 5):
+            load(g)
+
+        ident_f = keep.tile([P, P], F32, name="ident_f", align_bytes=64)
+        make_identity(nc, ident_f[:])
+        ident_b = keep.tile([P, P], BF16, name="ident_b", align_bytes=64)
+        make_identity(nc, ident_b[:])
+
+        gas, gacs, gass = {}, {}, {}
+
+        def a1(g, piece):
+            if piece == 0:
+                gas[g] = work.tile([P, 8, P64, 4], BF16, name="ga", tag="ga", bufs=3, align_bytes=64)
+            sl = slice(2 * piece, 2 * piece + 2)
+            nc.scalar.copy(out=gas[g][:, sl], in_=raws[g][:, sl].rearrange("q i j w -> q i w j"))
+
+        def a2(g):
+            c = work.tile([P, C], U32, name="gac", tag="gac", bufs=3, align_bytes=64)
+            s = work.tile([P, C], U8, name="gas", tag="gas", bufs=3, align_bytes=64)
+            nc.vector.quantize_mx(out=c[:].bitcast(E5M2), scales=s[:], in_=gas[g][:].rearrange("q i w j -> q (i w j)"))
+            gacs[g], gass[g] = c, s
+
+        dms = {}
+
+        def dm(g, ct):
+            t = psum.tile([P, C], F32, name="dm", tag="dm", bufs=2)
+            cols = slice(ct * P, (ct + 1) * P)
+            nc.tensor.matmul_mx(out=t[:], lhsT=w_codes[:, cols].bitcast(E4M3), lhsT_scale=w_scales[:, cols],
+                                rhs=gacs[g][:].bitcast(E5M2), rhs_scale=gass[g][:], start=True, stop=True)
+            dms[g, ct] = t
+
+        accs = {}
+
+        def fma(g, ct):
+            b, oct_ = g // 4, g % 4
+            if oct_ == 0 and ct == 0:
+                accs[b] = work.tile([P, 4, 4, P64], F32, name="acc", tag="acc", bufs=2, align_bytes=64)
+            acc = accs[b]
+            for i in range(8):
+                src = dms[g, ct][:, i * P64:(i + 1) * P64]
+                sc = qt[:, ct, g * 8 + i:g * 8 + i + 1]
+                dst = acc[:, ct, i % 4, :]
+                if oct_ == 0 and i < 4:
+                    nc.vector.tensor_scalar(out=dst, in0=src, scalar1=sc, scalar2=None, op0=MULT)
+                else:
+                    nc.vector.scalar_tensor_tensor(out=dst, in0=src, scalar=sc, in1=dst, op0=MULT, op1=ADD)
+
+        def finish(b):
+            acc = accs[b]
+            h = work.tile([P, 4, 2, P64], F32, name="half", tag="half", bufs=2, align_bytes=64)
+            r = work.tile([P, 4, P64], F32, name="res0", tag="res0", bufs=2, align_bytes=64)
+            nc.vector.tensor_tensor(out=h[:], in0=acc[:, :, 0:2, :], in1=acc[:, :, 2:4, :], op=ADD)
+            nc.vector.tensor_tensor(out=r[:], in0=h[:, :, 0, :], in1=h[:, :, 1, :], op=ADD)
+            nc.sync.dma_start(out=out_0[b].rearrange("(m k) y x -> m (k y x)", k=4), in_=r[:].rearrange("m k w -> m (k w)"))
+
+        rs, gbs = {}, {}
+
+        def b1(g, u):
+            if u == 0:
+                rs[g] = work.tile([P, 2, 4, P], F32, name="rw", tag="rw", bufs=2, align_bytes=64)
+            words = raws[g][:].rearrange("q i j w -> q (i j w)").bitcast(F32).rearrange(
+                "q (i j h u) -> q u j i h", i=8, j=4, u=2)
+            for_j = rs[g][:, u].rearrange("q j (i h) -> q j i h", i=8)
+            nc.scalar.copy(out=for_j, in_=words[:, u])
+
+        trs = {}
+
+        def b2(g):
+            for jh in range(2):
+                t = psum.tile([P, 2, 2, P], F32, name="tr", tag="tr", bufs=2)
+                for j2 in range(2):
+                    for u in range(2):
+                        nc.tensor.transpose(t[:, j2, u, :], rs[g][:, u, 2 * jh + j2, :], ident_f[:])
+                trs[g, jh] = t
+
+        def b3(g, jh):
+            if jh == 0:
+                gbs[g] = work.tile([P, 4, P, 4], BF16, name="gb", tag="gb", bufs=2, align_bytes=64)
+            dst = gbs[g][:, 2 * jh:2 * jh + 2].rearrange("t j q e -> t (j q e)").bitcast(F32).rearrange(
+                "t (j q u) -> t j q u", j=2, u=2)
+            nc.scalar.copy(out=dst, in_=trs[g, jh][:].rearrange("t j u q -> t j q u"))
+
+        gb_codes = keep.tile([P, PASSES, C], U32, name="gb_codes", align_bytes=64)
+        gb_scales = keep.tile([P, PASSES, C], U8, name="gb_scales", align_bytes=64)
+        mb_codes = keep.tile([P, PASSES, C], U32, name="mb_codes", align_bytes=64)
+        mb_scales = keep.tile([P, PASSES, C], U8, name="mb_scales", align_bytes=64)
+
+        def b4(g):
+            nc.vector.quantize_mx(out=gb_codes[:, g].bitcast(E5M2), scales=gb_scales[:, g],
+                                  in_=gbs[g][:].rearrange("t j q e -> t (j q e)"))
+
+        qbs, mbs, fbs, freps = {}, {}, {}, {}
+
+        def m1(g):
+            t = psum.tile([P, 2 * C], BF16, name="qb", tag="qb", bufs=1)
+            for h in range(2):
+                nc.tensor.matmul(t[:, h * C:(h + 1) * C], lhsT=spread[:, g * P:(g + 1) * P],
+                                 rhs=q_dup[:].rearrange("p c e -> p (c e)")[:, h * C:(h + 1) * C], start=True, stop=True)
+            qbs[g] = t
+
+        def m2(g):
+            t = work.tile([P, C, 2, 2], BF16, name="mb", tag="mb", bufs=2, align_bytes=64)
+            nc.vector.tensor_tensor(
+                out=t[:], in0=fbs[g // 4][:],
+                in1=qbs[g][:].rearrange("p (c e) -> p c e", e=2).unsqueeze(2).to_broadcast([P, C, 2, 2]), op=MULT)
+            mbs[g] = t
+
+        def m3(g):
+            nc.vector.quantize_mx(out=mb_codes[:, g].bitcast(E4M3), scales=mb_scales[:, g],
+                                  in_=mbs[g][:].rearrange("t c u e -> t (c u e)"))
+
+        def f1(b):
+            t = work.tile([P, 4, 2, 8, 16], F32, name="frep", tag="frep", bufs=1, align_bytes=64)
+            words = f_sb[:].rearrange("r k w -> r (k w)").bitcast(F32).rearrange("r (b k h u) -> r b u k h", b=4, k=4, u=2)
+            for u in range(2):
+                nc.scalar.copy(out=t[:, :, u], in_=words[:, b, u].unsqueeze(2).to_broadcast([P, 4, 8, 16]))
+            freps[b] = t
+
+        ftr = {}
+
+        def f2(b):
+            for kh in range(2):
+                t = psum.tile([P, 2, 2, P], F32, name="ftr", tag="tr", bufs=2)
+                for k2 in range(2):
+                    for u in range(2):
+                        nc.tensor.transpose(t[:, k2, u, :], freps[b][:, 2 * kh + k2, u].rearrange("r i h -> r (i h)"), ident_f[:])
+                ftr[b, kh] = t
+
+        def f3(b):
+            fbs[b] = work.tile([P, C, 2, 2], BF16, name="fb", tag="fb", bufs=2, align_bytes=64)
+            for kh in range(2):
+                dst = fbs[b][:, 2 * kh * P:(2 * kh + 2) * P].rearrange("t c u e -> t (c u e)").bitcast(F32).rearrange(
+                    "t (k r u) -> t k r u", k=2, u=2)
+                nc.scalar.copy(out=dst, in_=ftr[b, kh][:].rearrange("t k u r -> t k r u"))
+
+        out_acc = [psum.tile([P, C], F32, name="oacc%d" % j, tag="oacc%d" % j, bufs=1) for j in range(3)]
+
+        def o(g, js):
+            for j in js:
+                cols = slice(j * P, (j + 1) * P)
+                nc.tensor.matmul_mx(out=out_acc[j][:], lhsT=gb_codes[:, g, cols].bitcast(E5M2), lhsT_scale=gb_scales[:, g, cols],
+                                    rhs=mb_codes[:, g].bitcast(E4M3), rhs_scale=mb_scales[:, g],
+                                    start=(g == 0), stop=(g == PASSES - 1))
+
+        for k in range(4):
+            a1(0, k)
+        w_grp = keep.tile([P, 4, P, 4], BF16, name="w_grp", align_bytes=64)
+        nc.vector.tensor_copy(out=w_grp[:], in_=w_raw[:].rearrange("q j (m k) -> q k m j", k=4))
+        a2(0)
+        w_codes = keep.tile([P, C], U32, name="w_codes", align_bytes=64)
+        w_scales = keep.tile([P, C], U8, name="w_scales", align_bytes=64)
+        nc.vector.quantize_mx(out=w_codes[:].bitcast(E4M3), scales=w_scales[:], in_=w_grp[:].rearrange("q k m j -> q (k m j)"))
+        q_sort = keep.tile([P, 4, P], BF16, name="q_sort", align_bytes=64)
+        nc.vector.tensor_copy(out=q_sort[:], in_=q_sb[:].rearrange("p (m k) -> p k m", k=4))
+        qt_ps = psum.tile([P, 4, P], BF16, name="qt_ps", tag="tr", bufs=2)
+        for ct in range(4):
+            nc.tensor.transpose(qt_ps[:, ct, :], q_sort[:, ct, :], ident_b[:])
+        qt = keep.tile([P, 4, P], F32, name="qt", align_bytes=64)
+        nc.vector.tensor_copy(out=qt[:], in_=qt_ps[:])
+        dm(0, 0)
+        dm(0, 1)
+        q_dup = keep.tile([P, C, 2], BF16, name="q_dup", align_bytes=64)
+        spread = keep.tile([P, P * 16], BF16, name="spread", align_bytes=64)
+        for k in range(4):
+            a1(1, k)
+        f1(0)
+
+        LAST = PASSES - 1
+        for s in range(PASSES + 3):
+            if s + 5 < PASSES:
+                load(s + 5)
+            fp = s // 4 + 1
+            if 0 < s <= LAST:
+                dm(s, 1)
+            if s <= LAST:
+                fma(s, 0)
+                if s + 1 <= LAST:
+                    a2(s + 1)
+            if 0 <= s - 1 <= LAST:
+                b2(s - 1)
+            if s == 0:
+                f2(0)
+            if s + 2 <= LAST:
+                a1(s + 2, 0)
+            if 0 <= s - 1 <= LAST:
+                b3(s - 1, 0)
+            if s == 0:
+                f3(0)
+            if s + 2 <= LAST:
+                a1(s + 2, 1)
+            if 0 <= s - 1 <= LAST:
+                b3(s - 1, 1)
+            if s <= LAST:
+                dm(s, 2)
+                fma(s, 1)
+            if s == 0:
+                nc.vector.tensor_copy(out=q_dup[:], in_=q_sb[:].unsqueeze(2).to_broadcast([P, C, 2]))
+                nc.vector.tensor_copy(out=spread[:].rearrange("p (k r) -> p k r", r=16), in_=ident_b[:].unsqueeze(2).to_broadcast([P, P, 16]))
+            if 0 <= s - 2 <= LAST:
+                m2(s - 2)
+            if 0 <= s - 3 <= LAST:
+                o(s - 3, range(3))
+            if s == PASSES:
+                out_acc.append(psum.tile([P, C], F32, name="oacc3", tag="dm", bufs=2))
+                for g in range(0, PASSES - 3 + 1):
+                    o(g, [3])
+            if s > PASSES:
+                o(s - 3, [3])
+            if s <= LAST:
+                dm(s, 3)
+                fma(s, 2)
+            if s + 2 <= LAST:
+                a1(s + 2, 2)
+            if s <= LAST:
+                b1(s, 0)
+            if 0 <= s - 2 <= LAST:
+                b4(s - 2)
+            if s + 2 <= LAST:
+                a1(s + 2, 3)
+            if s <= LAST:
+                b1(s, 1)
+            if 0 <= s - 1 <= LAST:
+                m1(s - 1)
+            if s + 1 <= LAST:
+                dm(s + 1, 0)
+            if s <= LAST:
+                fma(s, 3)
+            if 0 <= s - 2 <= LAST:
+                m3(s - 2)
+            if s % 4 == 3 and s <= LAST:
+                finish(s // 4)
+            if s % 4 == 2 and fp < B:
+                f1(fp)
+            if s % 4 == 3 and fp < B:
+                f2(fp)
+                f3(fp)
+
+        res1 = keep.tile([P, 4, C], F32, name="res1", align_bytes=64)
+        rows = out_1.rearrange("(q j) c -> q j c", j=4)
+        for j in range(4):
+            if j % 2 == 0:
+                nc.scalar.copy(out=res1[:, j], in_=out_acc[j][:])
+            else:
+                nc.vector.tensor_copy(out=res1[:, j], in_=out_acc[j][:])
+            nc.sync.dma_start(out=rows[:, j], in_=res1[:, j])

@@ -16,6 +16,8 @@ E4M3 = mybir.dt.float8_e4m3fn_x4
 E5M2 = mybir.dt.float8_e5m2_x4
 ADD = mybir.AluOpType.add
 MULT = mybir.AluOpType.mult
+COPY = mybir.ActivationFunctionType.Copy
+AX = mybir.AxisListType.X
 P = 128
 
 
@@ -30,7 +32,7 @@ def tile_rpn_modulator_pb_v_kernel(tc, q, feats, po_w, po_b, grad_out, out_0, ou
         raws = {}
 
         def load(g, pieces=1):
-            t = work.tile([P, 8, 4, P64], BF16, name="raw", tag="raw", bufs=8, align_bytes=64)
+            t = work.tile([P, 8, 4, P64], BF16, name="raw", tag="raw", bufs=10, align_bytes=64)
             b, i0 = g // 4, 8 * (g % 4)
             n = 8 // pieces
             for k in range(pieces):
@@ -39,255 +41,318 @@ def tile_rpn_modulator_pb_v_kernel(tc, q, feats, po_w, po_b, grad_out, out_0, ou
                     in_=grad_out[b, i0 + k * n:i0 + (k + 1) * n].rearrange("i (q j) y x -> q i (j y x)", j=4))
             raws[g] = t
 
-        load(0, 4)
-        w_raw = keep.tile([P, 4, C], BF16, name="w_raw", align_bytes=64)
-        nc.sync.dma_start(out=w_raw[:], in_=po_w.rearrange("(q j) c -> q j c", j=4))
         q_sb = keep.tile([P, C], BF16, name="q_sb", align_bytes=64)
         nc.sync.dma_start(out=q_sb[:], in_=q.rearrange("b i c -> (b i) c"))
+        load(0, 2)
+        w_raw = keep.tile([P, 4, C], BF16, name="w_raw", align_bytes=64)
+        nc.sync.dma_start(out=w_raw[:], in_=po_w.rearrange("(q j) c -> q j c", j=4))
         load(1)
-        f_sb = keep.tile([P, 16, P64], BF16, name="f_sb", align_bytes=64)
-        nc.sync.dma_start(out=f_sb[:], in_=feats.rearrange("b (k r) y x -> r (b k) (y x)", r=P))
-        for g in range(2, 5):
-            load(g)
+        load(2)
+        load(3)
+        load(4)
 
         ident_f = keep.tile([P, P], F32, name="ident_f", align_bytes=64)
         make_identity(nc, ident_f[:])
         ident_b = keep.tile([P, P], BF16, name="ident_b", align_bytes=64)
         make_identity(nc, ident_b[:])
 
+        q_dup = keep.tile([P, C, 2], BF16, name="q_dup", align_bytes=64)
+        nc.vector.tensor_copy(out=q_dup[:], in_=q_sb[:].unsqueeze(2).to_broadcast([P, C, 2]))
+        q_sort = keep.tile([P, 4, P], BF16, name="q_sort", align_bytes=64)
+        nc.vector.tensor_copy(out=q_sort[:], in_=q_sb[:].rearrange("p (m k) -> p k m", k=4))
+        f_sb = keep.tile([P, 16, P64], BF16, name="f_sb", align_bytes=64)
+        nc.sync.dma_start(out=out_1[0:P, :], in_=q_dup[:].rearrange("p c e -> p (c e)").bitcast(F32))
+        q_all = keep.tile([P, PASSES, C], F32, name="q_all", align_bytes=64)
+        parked = out_1[0:P, :].rearrange("(g i) c -> i g c", i=8)
+
+        def load_q(g0, g1):
+            for i in range(8):
+                nc.sync.dma_start(out=q_all[16 * i:16 * (i + 1), g0:g1, :],
+                                  in_=parked[i, g0:g1, :].unsqueeze(0).to_broadcast([16, g1 - g0, C]))
+
+        load(5)
+        nc.sync.dma_start(out=f_sb[:], in_=feats.rearrange("b (k r) y x -> r (b k) (y x)", r=P))
+        load(6)
+        load_q(0, 4)
+        load(7)
+
         gas, gacs, gass = {}, {}, {}
 
-        def a1(g, piece):
-            if piece == 0:
+        def a1(g, half, eng):
+            if half == 0:
                 gas[g] = work.tile([P, 8, P64, 4], BF16, name="ga", tag="ga", bufs=3, align_bytes=64)
-            sl = slice(2 * piece, 2 * piece + 2)
-            nc.scalar.copy(out=gas[g][:, sl], in_=raws[g][:, sl].rearrange("q i j w -> q i w j"))
+            sl = slice(4 * half, 4 * half + 4)
+            src = raws[g][:, sl].rearrange("q i j w -> q i w j")
+            if eng == "v":
+                nc.vector.tensor_copy(out=gas[g][:, sl], in_=src)
+            else:
+                nc.scalar.copy(out=gas[g][:, sl], in_=src)
 
         def a2(g):
-            c = work.tile([P, C], U32, name="gac", tag="gac", bufs=3, align_bytes=64)
-            s = work.tile([P, C], U8, name="gas", tag="gas", bufs=3, align_bytes=64)
+            c = work.tile([P, C], U32, name="gac", tag="gac", bufs=8, align_bytes=64)
+            s = work.tile([P, C], U8, name="gsc", tag="gsc", bufs=8, align_bytes=64)
             nc.vector.quantize_mx(out=c[:].bitcast(E5M2), scales=s[:], in_=gas[g][:].rearrange("q i w j -> q (i w j)"))
             gacs[g], gass[g] = c, s
 
-        dms = {}
+        def unit(k):
+            b = k // 16
+            ct, octet = (k % 4, k // 4) if b == 0 else ((k // 4) % 4, k % 4)
+            return b, ct, octet, 4 * b + octet
 
-        def dm(g, ct):
-            t = psum.tile([P, C], F32, name="dm", tag="dm", bufs=2)
+        dms, prods, daccs, dsums = {}, {}, {}, {}
+
+        def dm(k):
+            b, ct, octet, g = unit(k)
+            t = psum.tile([P, C], F32, name="dm", tag="x", bufs=3)
             cols = slice(ct * P, (ct + 1) * P)
             nc.tensor.matmul_mx(out=t[:], lhsT=w_codes[:, cols].bitcast(E4M3), lhsT_scale=w_scales[:, cols],
                                 rhs=gacs[g][:].bitcast(E5M2), rhs_scale=gass[g][:], start=True, stop=True)
-            dms[g, ct] = t
+            dms[k] = t
 
-        accs = {}
+        def prod(k, eng):
+            b, ct, octet, g = unit(k)
+            t = work.tile([P, 8, P64], F32, name="prod", tag="prod", bufs=8, align_bytes=64)
+            if eng == "v":
+                nc.vector.tensor_tensor(out=t[:], in0=dms[k][:].rearrange("c (i w) -> c i w", i=8),
+                                        in1=qt[:, ct, 8 * g:8 * g + 8].unsqueeze(2).to_broadcast([P, 8, P64]), op=MULT)
+            else:
+                for i in range(8):
+                    nc.scalar.activation(out=t[:, i, :], in_=dms[k][:, i * P64:(i + 1) * P64], func=COPY,
+                                         scale=qt[:, ct, 8 * g + i:8 * g + i + 1])
+            prods[k] = t
 
-        def fma(g, ct):
-            b, oct_ = g // 4, g % 4
-            if oct_ == 0 and ct == 0:
-                accs[b] = work.tile([P, 4, 4, P64], F32, name="acc", tag="acc", bufs=2, align_bytes=64)
-            acc = accs[b]
-            for i in range(8):
-                src = dms[g, ct][:, i * P64:(i + 1) * P64]
-                sc = qt[:, ct, g * 8 + i:g * 8 + i + 1]
-                dst = acc[:, ct, i % 4, :]
-                if oct_ == 0 and i < 4:
-                    nc.vector.tensor_scalar(out=dst, in0=src, scalar1=sc, scalar2=None, op0=MULT)
+        def acct(k):
+            b, ct, octet, g = unit(k)
+            if octet == 0 and (b == 0 or ct == 0):
+                if b == 0:
+                    daccs[b, ct] = psum.tile([P, P], F32, name="dacc0", tag="oacc%d" % ct, bufs=1)
                 else:
-                    nc.vector.scalar_tensor_tensor(out=dst, in0=src, scalar=sc, in1=dst, op0=MULT, op1=ADD)
+                    t = psum.tile([P, 4, P], F32, name="dacc", tag="dacc", bufs=1)
+                    dfull[b] = t[:]
+                    for j in range(4):
+                        daccs[b, j] = t[:, j]
+            for h in range(4):
+                nc.tensor.matmul(daccs[b, ct][:], lhsT=prods[k][:, 2 * h:2 * h + 2].rearrange("c i w -> c (i w)"),
+                                 rhs=ident_f[:], is_transpose=True, start=(octet == 0 and h == 0), stop=(octet == 3 and h == 3))
 
-        def finish(b):
-            acc = accs[b]
-            h = work.tile([P, 4, 2, P64], F32, name="half", tag="half", bufs=2, align_bytes=64)
+        def fin_s(b):
+            dsums[b] = work.tile([P, 4, P], F32, name="dsum", tag="dsum", bufs=2, align_bytes=64)
+            if b == 0:
+                for ct in range(4):
+                    nc.scalar.copy(out=dsums[b][:, ct], in_=daccs[b, ct][:])
+            else:
+                nc.scalar.copy(out=dsums[b][:], in_=dfull[b])
+
+        dfull = {}
+        backs = {}
+
+        def fin_t(b):
+            t = psum.tile([P, 4, P], F32, name="back", tag="x", bufs=3)
+            for ct in range(4):
+                nc.tensor.transpose(t[:, ct, :], dsums[b][:, ct, :], ident_f[:])
+            backs[b] = t
+
+        halves = {}
+
+        def fin_h(b):
+            halves[b] = work.tile([P, 4, P], F32, name="half", tag="half", bufs=2, align_bytes=64)
+            nc.scalar.copy(out=halves[b][:], in_=backs[b][:])
+
+        def fin_v(b):
             r = work.tile([P, 4, P64], F32, name="res0", tag="res0", bufs=2, align_bytes=64)
-            nc.vector.tensor_tensor(out=h[:], in0=acc[:, :, 0:2, :], in1=acc[:, :, 2:4, :], op=ADD)
-            nc.vector.tensor_tensor(out=r[:], in0=h[:, :, 0, :], in1=h[:, :, 1, :], op=ADD)
+            nc.vector.tensor_tensor(out=r[:], in0=halves[b][:, :, 0:P64], in1=halves[b][:, :, P64:P], op=ADD)
             nc.sync.dma_start(out=out_0[b].rearrange("(m k) y x -> m (k y x)", k=4), in_=r[:].rearrange("m k w -> m (k w)"))
 
-        rs, gbs = {}, {}
+        rs, gbs, trs = {}, {}, {}
 
-        def b1(g, u):
+        def b1(g, u, eng):
             if u == 0:
                 rs[g] = work.tile([P, 2, 4, P], F32, name="rw", tag="rw", bufs=2, align_bytes=64)
             words = raws[g][:].rearrange("q i j w -> q (i j w)").bitcast(F32).rearrange(
                 "q (i j h u) -> q u j i h", i=8, j=4, u=2)
-            for_j = rs[g][:, u].rearrange("q j (i h) -> q j i h", i=8)
-            nc.scalar.copy(out=for_j, in_=words[:, u])
+            dst = rs[g][:, u].rearrange("q j (i h) -> q j i h", i=8)
+            if eng == "v":
+                nc.vector.tensor_copy(out=dst, in_=words[:, u])
+            else:
+                nc.scalar.copy(out=dst, in_=words[:, u])
 
-        trs = {}
-
-        def b2(g):
-            for jh in range(2):
-                t = psum.tile([P, 2, 2, P], F32, name="tr", tag="tr", bufs=2)
-                for j2 in range(2):
-                    for u in range(2):
-                        nc.tensor.transpose(t[:, j2, u, :], rs[g][:, u, 2 * jh + j2, :], ident_f[:])
-                trs[g, jh] = t
+        def b2(g, jh):
+            t = psum.tile([P, 2, 2, P], F32, name="tr", tag="x", bufs=3)
+            for j2 in range(2):
+                for u in range(2):
+                    nc.tensor.transpose(t[:, j2, u, :], rs[g][:, u, 2 * jh + j2, :], ident_f[:])
+            trs[g, jh] = t
 
         def b3(g, jh):
             if jh == 0:
-                gbs[g] = work.tile([P, 4, P, 4], BF16, name="gb", tag="gb", bufs=2, align_bytes=64)
+                gbs[g] = work.tile([P, 4, P, 4], BF16, name="gb", tag="gb", bufs=3, align_bytes=64)
             dst = gbs[g][:, 2 * jh:2 * jh + 2].rearrange("t j q e -> t (j q e)").bitcast(F32).rearrange(
                 "t (j q u) -> t j q u", j=2, u=2)
             nc.scalar.copy(out=dst, in_=trs[g, jh][:].rearrange("t j u q -> t j q u"))
 
-        gb_codes = keep.tile([P, PASSES, C], U32, name="gb_codes", align_bytes=64)
-        gb_scales = keep.tile([P, PASSES, C], U8, name="gb_scales", align_bytes=64)
-        mb_codes = keep.tile([P, PASSES, C], U32, name="mb_codes", align_bytes=64)
-        mb_scales = keep.tile([P, PASSES, C], U8, name="mb_scales", align_bytes=64)
+        gbc, gbsc, mbc, mbsc, mbs = {}, {}, {}, {}, {}
 
         def b4(g):
-            nc.vector.quantize_mx(out=gb_codes[:, g].bitcast(E5M2), scales=gb_scales[:, g],
+            gbc[g] = work.tile([P, C], U32, name="gbc", tag="gbc", bufs=3, align_bytes=64)
+            gbsc[g] = work.tile([P, C], U8, name="gbsc", tag="gbsc", bufs=3, align_bytes=64)
+            nc.vector.quantize_mx(out=gbc[g][:].bitcast(E5M2), scales=gbsc[g][:],
                                   in_=gbs[g][:].rearrange("t j q e -> t (j q e)"))
-
-        qbs, mbs, fbs, freps = {}, {}, {}, {}
-
-        def m1(g):
-            t = psum.tile([P, 2 * C], BF16, name="qb", tag="qb", bufs=1)
-            for h in range(2):
-                nc.tensor.matmul(t[:, h * C:(h + 1) * C], lhsT=spread[:, g * P:(g + 1) * P],
-                                 rhs=q_dup[:].rearrange("p c e -> p (c e)")[:, h * C:(h + 1) * C], start=True, stop=True)
-            qbs[g] = t
 
         def m2(g):
             t = work.tile([P, C, 2, 2], BF16, name="mb", tag="mb", bufs=2, align_bytes=64)
             nc.vector.tensor_tensor(
                 out=t[:], in0=fbs[g // 4][:],
-                in1=qbs[g][:].rearrange("p (c e) -> p c e", e=2).unsqueeze(2).to_broadcast([P, C, 2, 2]), op=MULT)
+                in1=q_all[:, g].bitcast(BF16).rearrange("p (c e) -> p c e", e=2).unsqueeze(2).to_broadcast([P, C, 2, 2]), op=MULT)
             mbs[g] = t
 
         def m3(g):
-            nc.vector.quantize_mx(out=mb_codes[:, g].bitcast(E4M3), scales=mb_scales[:, g],
+            mbc[g] = work.tile([P, C], U32, name="mbc", tag="mbc", bufs=3, align_bytes=64)
+            mbsc[g] = work.tile([P, C], U8, name="mbsc", tag="mbsc", bufs=3, align_bytes=64)
+            nc.vector.quantize_mx(out=mbc[g][:].bitcast(E4M3), scales=mbsc[g][:],
                                   in_=mbs[g][:].rearrange("t c u e -> t (c u e)"))
+
+        freps, ftr, fbs = {}, {}, {}
 
         def f1(b):
             t = work.tile([P, 4, 2, 8, 16], F32, name="frep", tag="frep", bufs=1, align_bytes=64)
             words = f_sb[:].rearrange("r k w -> r (k w)").bitcast(F32).rearrange("r (b k h u) -> r b u k h", b=4, k=4, u=2)
             for u in range(2):
-                nc.scalar.copy(out=t[:, :, u], in_=words[:, b, u].unsqueeze(2).to_broadcast([P, 4, 8, 16]))
+                nc.vector.tensor_copy(out=t[:, :, u], in_=words[:, b, u].unsqueeze(2).to_broadcast([P, 4, 8, 16]))
             freps[b] = t
 
-        ftr = {}
+        def f2(b, kh):
+            t = psum.tile([P, 2, 2, P], F32, name="ftr", tag="x", bufs=3)
+            for k2 in range(2):
+                for u in range(2):
+                    nc.tensor.transpose(t[:, k2, u, :], freps[b][:, 2 * kh + k2, u].rearrange("r i h -> r (i h)"), ident_f[:])
+            ftr[b, kh] = t
 
-        def f2(b):
-            for kh in range(2):
-                t = psum.tile([P, 2, 2, P], F32, name="ftr", tag="tr", bufs=2)
-                for k2 in range(2):
-                    for u in range(2):
-                        nc.tensor.transpose(t[:, k2, u, :], freps[b][:, 2 * kh + k2, u].rearrange("r i h -> r (i h)"), ident_f[:])
-                ftr[b, kh] = t
+        def f3(b, kh):
+            if kh == 0:
+                fbs[b] = work.tile([P, C, 2, 2], BF16, name="fb", tag="fb", bufs=3, align_bytes=64)
+            dst = fbs[b][:, 2 * kh * P:(2 * kh + 2) * P].rearrange("t c u e -> t (c u e)").bitcast(F32).rearrange(
+                "t (k r u) -> t k r u", k=2, u=2)
+            nc.scalar.copy(out=dst, in_=ftr[b, kh][:].rearrange("t k u r -> t k r u"))
 
-        def f3(b):
-            fbs[b] = work.tile([P, C, 2, 2], BF16, name="fb", tag="fb", bufs=2, align_bytes=64)
-            for kh in range(2):
-                dst = fbs[b][:, 2 * kh * P:(2 * kh + 2) * P].rearrange("t c u e -> t (c u e)").bitcast(F32).rearrange(
-                    "t (k r u) -> t k r u", k=2, u=2)
-                nc.scalar.copy(out=dst, in_=ftr[b, kh][:].rearrange("t k u r -> t k r u"))
-
-        out_acc = [psum.tile([P, C], F32, name="oacc%d" % j, tag="oacc%d" % j, bufs=1) for j in range(3)]
+        out_acc = {}
 
         def o(g, js):
             for j in js:
+                if g == 0:
+                    out_acc[j] = psum.tile([P, C], F32, name="oacc", tag="oacc%d" % j, bufs=1)
                 cols = slice(j * P, (j + 1) * P)
-                nc.tensor.matmul_mx(out=out_acc[j][:], lhsT=gb_codes[:, g, cols].bitcast(E5M2), lhsT_scale=gb_scales[:, g, cols],
-                                    rhs=mb_codes[:, g].bitcast(E4M3), rhs_scale=mb_scales[:, g],
+                nc.tensor.matmul_mx(out=out_acc[j][:], lhsT=gbc[g][:, cols].bitcast(E5M2), lhsT_scale=gbsc[g][:, cols],
+                                    rhs=mbc[g][:].bitcast(E4M3), rhs_scale=mbsc[g][:],
                                     start=(g == 0), stop=(g == PASSES - 1))
 
-        for k in range(4):
-            a1(0, k)
-        w_grp = keep.tile([P, 4, P, 4], BF16, name="w_grp", align_bytes=64)
-        nc.vector.tensor_copy(out=w_grp[:], in_=w_raw[:].rearrange("q j (m k) -> q k m j", k=4))
-        a2(0)
-        w_codes = keep.tile([P, C], U32, name="w_codes", align_bytes=64)
-        w_scales = keep.tile([P, C], U8, name="w_scales", align_bytes=64)
-        nc.vector.quantize_mx(out=w_codes[:].bitcast(E4M3), scales=w_scales[:], in_=w_grp[:].rearrange("q k m j -> q (k m j)"))
-        q_sort = keep.tile([P, 4, P], BF16, name="q_sort", align_bytes=64)
-        nc.vector.tensor_copy(out=q_sort[:], in_=q_sb[:].rearrange("p (m k) -> p k m", k=4))
-        qt_ps = psum.tile([P, 4, P], BF16, name="qt_ps", tag="tr", bufs=2)
+        def inter(g):
+            for part in range(2):
+                a1(g, part, "s" if g == 0 and part == 0 else "v")
+
+        LAST = PASSES - 1
+
+        def prep(g):
+            if g <= LAST:
+                inter(g)
+
+        def quant(g):
+            if g <= LAST:
+                a2(g)
+
+        qt_ps = psum.tile([P, 4, P], BF16, name="qt_ps", tag="x", bufs=3)
         for ct in range(4):
             nc.tensor.transpose(qt_ps[:, ct, :], q_sort[:, ct, :], ident_b[:])
         qt = keep.tile([P, 4, P], F32, name="qt", align_bytes=64)
         nc.vector.tensor_copy(out=qt[:], in_=qt_ps[:])
-        dm(0, 0)
-        dm(0, 1)
-        q_dup = keep.tile([P, C, 2], BF16, name="q_dup", align_bytes=64)
-        spread = keep.tile([P, P * 16], BF16, name="spread", align_bytes=64)
-        for k in range(4):
-            a1(1, k)
-        f1(0)
+        w_grp = keep.tile([P, 4, P, 4], BF16, name="w_grp", align_bytes=64)
+        w_codes = keep.tile([P, C], U32, name="w_codes", align_bytes=64)
+        w_scales = keep.tile([P, C], U8, name="w_scales", align_bytes=64)
+        inter(0)
+        nc.vector.tensor_copy(out=w_grp[:], in_=w_raw[:].rearrange("q j (m k) -> q k m j", k=4))
+        a2(0)
+        nc.vector.quantize_mx(out=w_codes[:].bitcast(E4M3), scales=w_scales[:], in_=w_grp[:].rearrange("q k m j -> q (k m j)"))
 
-        LAST = PASSES - 1
-        for s in range(PASSES + 3):
-            if s + 5 < PASSES:
-                load(s + 5)
-            fp = s // 4 + 1
-            if 0 < s <= LAST:
-                dm(s, 1)
-            if s <= LAST:
-                fma(s, 0)
-                if s + 1 <= LAST:
-                    a2(s + 1)
-            if 0 <= s - 1 <= LAST:
-                b2(s - 1)
-            if s == 0:
-                f2(0)
-            if s + 2 <= LAST:
-                a1(s + 2, 0)
-            if 0 <= s - 1 <= LAST:
-                b3(s - 1, 0)
-            if s == 0:
-                f3(0)
-            if s + 2 <= LAST:
-                a1(s + 2, 1)
-            if 0 <= s - 1 <= LAST:
-                b3(s - 1, 1)
-            if s <= LAST:
-                dm(s, 2)
-                fma(s, 1)
-            if s == 0:
-                nc.vector.tensor_copy(out=q_dup[:], in_=q_sb[:].unsqueeze(2).to_broadcast([P, C, 2]))
-                nc.vector.tensor_copy(out=spread[:].rearrange("p (k r) -> p k r", r=16), in_=ident_b[:].unsqueeze(2).to_broadcast([P, P, 16]))
-            if 0 <= s - 2 <= LAST:
-                m2(s - 2)
-            if 0 <= s - 3 <= LAST:
-                o(s - 3, range(3))
-            if s == PASSES:
-                out_acc.append(psum.tile([P, C], F32, name="oacc3", tag="dm", bufs=2))
-                for g in range(0, PASSES - 3 + 1):
-                    o(g, [3])
-            if s > PASSES:
-                o(s - 3, [3])
-            if s <= LAST:
-                dm(s, 3)
-                fma(s, 2)
-            if s + 2 <= LAST:
-                a1(s + 2, 2)
-            if s <= LAST:
-                b1(s, 0)
-            if 0 <= s - 2 <= LAST:
-                b4(s - 2)
-            if s + 2 <= LAST:
-                a1(s + 2, 3)
-            if s <= LAST:
-                b1(s, 1)
-            if 0 <= s - 1 <= LAST:
-                m1(s - 1)
-            if s + 1 <= LAST:
-                dm(s + 1, 0)
-            if s <= LAST:
-                fma(s, 3)
-            if 0 <= s - 2 <= LAST:
-                m3(s - 2)
-            if s % 4 == 3 and s <= LAST:
-                finish(s // 4)
-            if s % 4 == 2 and fp < B:
-                f1(fp)
-            if s % 4 == 3 and fp < B:
-                f2(fp)
-                f3(fp)
+        def on_v(k):
+            return False
 
+        def pd(k, eng):
+            dm(k)
+            prod(k, eng)
+
+        early = {0: (1, 2), 1: (3, 4), 2: (5, 6), 3: (7,)}
+        BL = 2
+        STEPS = PASSES + BL + 3
+        for s in range(STEPS):
+            j = s - BL
+            D = s < PASSES
+            a_new = early.get(s, (s + 4,) if s + 4 <= LAST else ())
+            if s + 6 + 2 <= LAST and s + 6 + 2 > 7:
+                load(s + 6 + 2)
+            if s == 2:
+                load_q(4, PASSES)
+            pk = 4 * (s - 1)
+            P0 = 1 <= s <= PASSES
+            if P0:
+                acct(pk)
+                acct(pk + 1)
+            if 0 <= j - 1 <= LAST:
+                b2(j - 1, 0)
+                b2(j - 1, 1)
+                b3(j - 1, 0)
+                b3(j - 1, 1)
+            if P0:
+                acct(pk + 2)
+                acct(pk + 3)
+            if s == 4:
+                fin_s(0)
+            if s > 4 and s % 4 == 0 and s <= PASSES:
+                fin_s(s // 4 - 1)
+            if 5 <= s <= PASSES + 1 and s % 4 == 1:
+                fin_t(s // 4 - 1)
+                fin_h(s // 4 - 1)
+            if 0 <= j <= LAST:
+                b1(j, 0, "s" if False else "v")
+                b1(j, 1, "v")
+            for g in a_new:
+                prep(g)
+            if D:
+                pd(4 * s, "v" if on_v(4 * s) else "s")
+                pd(4 * s + 1, "v" if on_v(4 * s + 1) else "s")
+            if 0 <= j - 2 <= LAST:
+                b4(j - 2)
+                m2(j - 2)
+            if 0 <= j - 3 <= LAST:
+                o(j - 3, (0, 1))
+            for g in a_new:
+                quant(g)
+            if D:
+                pd(4 * s + 2, "v" if on_v(4 * s + 2) else "s")
+                pd(4 * s + 3, "v" if on_v(4 * s + 3) else "s")
+            if 0 <= j - 3 <= LAST:
+                o(j - 3, (2, 3))
+            if 0 <= j - 2 <= LAST:
+                m3(j - 2)
+            if 6 <= s and s % 4 == 2 and s <= PASSES + 2:
+                fin_v(s // 4 - 1)
+            if s == 1:
+                f1(0)
+            if s == 2:
+                f2(0, 0)
+                f3(0, 0)
+                f2(0, 1)
+                f3(0, 1)
+            if s % 4 == 3 and s < 12:
+                f1(s // 4 + 1)
+            if s % 4 == 0 and 0 < s < 16:
+                f2(s // 4, 0)
+                f3(s // 4, 0)
+            if s % 4 == 1 and 1 < s < 16:
+                f2(s // 4, 1)
+                f3(s // 4, 1)
         res1 = keep.tile([P, 4, C], F32, name="res1", align_bytes=64)
         rows = out_1.rearrange("(q j) c -> q j c", j=4)
         for j in range(4):
-            if j % 2 == 0:
+            if j % 2 == 1:
                 nc.scalar.copy(out=res1[:, j], in_=out_acc[j][:])
             else:
                 nc.vector.tensor_copy(out=res1[:, j], in_=out_acc[j][:])

@@ -31,8 +31,19 @@ def tile_rpn_modulator_pb_v_kernel(tc, q, feats, po_w, po_b, grad_out, out_0, ou
 
         raws = {}
 
+        def by_o(g):
+            return False
+
         def load(g, pieces=1):
-            t = work.tile([P, 8, 4, P64], BF16, name="raw", tag="raw", bufs=10, align_bytes=64)
+            if by_o(g):
+                t = work.tile([P, 4, 8, P64], BF16, name="raw", tag="raw", bufs=9, align_bytes=64)
+                b, i0 = g // 4, 8 * (g % 4)
+                for j in range(4):
+                    nc.sync.dma_start(
+                        out=t[:, j], in_=grad_out[b, i0:i0 + 8].rearrange("i (q j) y x -> j q i (y x)", j=4)[j])
+                raws[g] = t
+                return
+            t = work.tile([P, 8, 4, P64], BF16, name="raw", tag="raw", bufs=9, align_bytes=64)
             b, i0 = g // 4, 8 * (g % 4)
             n = 8 // pieces
             for k in range(pieces):
@@ -63,18 +74,15 @@ def tile_rpn_modulator_pb_v_kernel(tc, q, feats, po_w, po_b, grad_out, out_0, ou
         f_sb = keep.tile([P, 16, P64], BF16, name="f_sb", align_bytes=64)
         nc.sync.dma_start(out=out_1[0:P, :], in_=q_dup[:].rearrange("p c e -> p (c e)").bitcast(F32))
         q_all = keep.tile([P, PASSES, C], F32, name="q_all", align_bytes=64)
-        parked = out_1[0:P, :].rearrange("(g i) c -> i g c", i=8)
-
-        def load_q(g0, g1):
-            for i in range(8):
-                nc.sync.dma_start(out=q_all[16 * i:16 * (i + 1), g0:g1, :],
-                                  in_=parked[i, g0:g1, :].unsqueeze(0).to_broadcast([16, g1 - g0, C]))
+        def load_q(g):
+            nc.sync.dma_start(out=q_all[:, g, :], in_=out_1[8 * g:8 * g + 8, :].unsqueeze(1).to_broadcast([8, 16, C]))
 
         load(5)
         nc.sync.dma_start(out=f_sb[:], in_=feats.rearrange("b (k r) y x -> r (b k) (y x)", r=P))
         load(6)
-        load_q(0, 4)
         load(7)
+        load_q(0)
+        load_q(1)
 
         gas, gacs, gass = {}, {}, {}
 
@@ -82,11 +90,17 @@ def tile_rpn_modulator_pb_v_kernel(tc, q, feats, po_w, po_b, grad_out, out_0, ou
             if half == 0:
                 gas[g] = work.tile([P, 8, P64, 4], BF16, name="ga", tag="ga", bufs=3, align_bytes=64)
             sl = slice(4 * half, 4 * half + 4)
-            src = raws[g][:, sl].rearrange("q i j w -> q i w j")
-            if eng == "v":
-                nc.vector.tensor_copy(out=gas[g][:, sl], in_=src)
+            if by_o(g):
+                src = raws[g][:, :, sl].rearrange("q j i w -> q j (i w)")
+                src = src.rearrange("q j t -> q t j")
+                dst = gas[g][:, sl].rearrange("q i w j -> q (i w) j")
             else:
-                nc.scalar.copy(out=gas[g][:, sl], in_=src)
+                src = raws[g][:, sl].rearrange("q i j w -> q i w j")
+                dst = gas[g][:, sl]
+            if eng == "v":
+                nc.vector.tensor_copy(out=dst, in_=src)
+            else:
+                nc.scalar.copy(out=dst, in_=src)
 
         def a2(g):
             c = work.tile([P, C], U32, name="gac", tag="gac", bufs=8, align_bytes=64)
@@ -166,6 +180,8 @@ def tile_rpn_modulator_pb_v_kernel(tc, q, feats, po_w, po_b, grad_out, out_0, ou
         rs, gbs, trs = {}, {}, {}
 
         def b1(g, u, eng):
+            if by_o(g):
+                return
             if u == 0:
                 rs[g] = work.tile([P, 2, 4, P], F32, name="rw", tag="rw", bufs=2, align_bytes=64)
             words = raws[g][:].rearrange("q i j w -> q (i j w)").bitcast(F32).rearrange(
@@ -180,7 +196,8 @@ def tile_rpn_modulator_pb_v_kernel(tc, q, feats, po_w, po_b, grad_out, out_0, ou
             t = psum.tile([P, 2, 2, P], F32, name="tr", tag="x", bufs=3)
             for j2 in range(2):
                 for u in range(2):
-                    nc.tensor.transpose(t[:, j2, u, :], rs[g][:, u, 2 * jh + j2, :], ident_f[:])
+                    pairs = raws[g][:, 2 * jh + j2].rearrange("q i w -> q (i w)").bitcast(F32)[:, u::2] if by_o(g) else rs[g][:, u, 2 * jh + j2, :]
+                    nc.tensor.transpose(t[:, j2, u, :], pairs, ident_f[:])
             trs[g, jh] = t
 
         def b3(g, jh):
@@ -286,10 +303,10 @@ def tile_rpn_modulator_pb_v_kernel(tc, q, feats, po_w, po_b, grad_out, out_0, ou
             j = s - BL
             D = s < PASSES
             a_new = early.get(s, (s + 4,) if s + 4 <= LAST else ())
-            if s + 6 + 2 <= LAST and s + 6 + 2 > 7:
-                load(s + 6 + 2)
-            if s == 2:
-                load_q(4, PASSES)
+            if s + 5 + 2 <= LAST and s + 5 + 2 > 7:
+                load(s + 5 + 2)
+            if s + 2 <= LAST:
+                load_q(s + 2)
             pk = 4 * (s - 1)
             P0 = 1 <= s <= PASSES
             if P0:

@@ -36,14 +36,14 @@ def tile_rpn_modulator_pb_v_kernel(tc, q, feats, po_w, po_b, grad_out, out_0, ou
 
         def load(g, pieces=1):
             if by_o(g):
-                t = work.tile([P, 4, 8, P64], BF16, name="raw", tag="raw", bufs=9, align_bytes=64)
+                t = work.tile([P, 4, 8, P64], BF16, name="raw", tag="raw", bufs=8, align_bytes=64)
                 b, i0 = g // 4, 8 * (g % 4)
                 for j in range(4):
                     nc.sync.dma_start(
                         out=t[:, j], in_=grad_out[b, i0:i0 + 8].rearrange("i (q j) y x -> j q i (y x)", j=4)[j])
                 raws[g] = t
                 return
-            t = work.tile([P, 8, 4, P64], BF16, name="raw", tag="raw", bufs=9, align_bytes=64)
+            t = work.tile([P, 8, 4, P64], BF16, name="raw", tag="raw", bufs=8, align_bytes=64)
             b, i0 = g // 4, 8 * (g % 4)
             n = 8 // pieces
             for k in range(pieces):
@@ -54,9 +54,9 @@ def tile_rpn_modulator_pb_v_kernel(tc, q, feats, po_w, po_b, grad_out, out_0, ou
 
         q_sb = keep.tile([P, C], BF16, name="q_sb", align_bytes=64)
         nc.sync.dma_start(out=q_sb[:], in_=q.rearrange("b i c -> (b i) c"))
-        load(0, 2)
         w_raw = keep.tile([P, 4, C], BF16, name="w_raw", align_bytes=64)
         nc.sync.dma_start(out=w_raw[:], in_=po_w.rearrange("(q j) c -> q j c", j=4))
+        load(0, 2)
         load(1)
         load(2)
         load(3)
@@ -73,14 +73,16 @@ def tile_rpn_modulator_pb_v_kernel(tc, q, feats, po_w, po_b, grad_out, out_0, ou
         nc.vector.tensor_copy(out=q_sort[:], in_=q_sb[:].rearrange("p (m k) -> p k m", k=4))
         f_sb = keep.tile([P, 16, P64], BF16, name="f_sb", align_bytes=64)
         nc.sync.dma_start(out=out_1[0:P, :], in_=q_dup[:].rearrange("p c e -> p (c e)").bitcast(F32))
-        q_all = keep.tile([P, PASSES, C], F32, name="q_all", align_bytes=64)
+        qspread = {}
+
         def load_q(g):
-            nc.sync.dma_start(out=q_all[:, g, :], in_=out_1[8 * g:8 * g + 8, :].unsqueeze(1).to_broadcast([8, 16, C]))
+            qspread[g] = work.tile([P, C], F32, name="qsp", tag="qsp", bufs=5, align_bytes=64)
+            nc.sync.dma_start(out=qspread[g][:], in_=out_1[8 * g:8 * g + 8, :].unsqueeze(1).to_broadcast([8, 16, C]))
 
         load(5)
-        nc.sync.dma_start(out=f_sb[:], in_=feats.rearrange("b (k r) y x -> r (b k) (y x)", r=P))
         load(6)
         load(7)
+        nc.sync.dma_start(out=f_sb[:], in_=feats.rearrange("b (k r) y x -> r (b k) (y x)", r=P))
         load_q(0)
         load_q(1)
 
@@ -88,15 +90,15 @@ def tile_rpn_modulator_pb_v_kernel(tc, q, feats, po_w, po_b, grad_out, out_0, ou
 
         def a1(g, half, eng):
             if half == 0:
-                gas[g] = work.tile([P, 8, P64, 4], BF16, name="ga", tag="ga", bufs=3, align_bytes=64)
+                gas[g] = work.tile([P, 8, P64, 4], BF16, name="ga", tag="ga", bufs=2, align_bytes=64)
             sl = slice(4 * half, 4 * half + 4)
             if by_o(g):
                 src = raws[g][:, :, sl].rearrange("q j i w -> q j (i w)")
-                src = src.rearrange("q j t -> q t j")
-                dst = gas[g][:, sl].rearrange("q i w j -> q (i w) j")
+                src = src.rearrange("q j (c k) -> q c j k", k=4)
+                dst = gas[g][:, sl].rearrange("q i w j -> q (i w) j").rearrange("q (c k) j -> q c j k", k=4)
             else:
-                src = raws[g][:, sl].rearrange("q i j w -> q i w j")
-                dst = gas[g][:, sl]
+                src = raws[g][:, sl].rearrange("q i j (c k) -> q i c j k", k=4)
+                dst = gas[g][:, sl].rearrange("q i (c k) j -> q i c j k", k=4)
             if eng == "v":
                 nc.vector.tensor_copy(out=dst, in_=src)
             else:
@@ -117,7 +119,7 @@ def tile_rpn_modulator_pb_v_kernel(tc, q, feats, po_w, po_b, grad_out, out_0, ou
 
         def dm(k):
             b, ct, octet, g = unit(k)
-            t = psum.tile([P, C], F32, name="dm", tag="x", bufs=3)
+            t = psum.tile([P, C], F32, name="dm", tag="x", bufs=4)
             cols = slice(ct * P, (ct + 1) * P)
             nc.tensor.matmul_mx(out=t[:], lhsT=w_codes[:, cols].bitcast(E4M3), lhsT_scale=w_scales[:, cols],
                                 rhs=gacs[g][:].bitcast(E5M2), rhs_scale=gass[g][:], start=True, stop=True)
@@ -125,7 +127,7 @@ def tile_rpn_modulator_pb_v_kernel(tc, q, feats, po_w, po_b, grad_out, out_0, ou
 
         def prod(k, eng):
             b, ct, octet, g = unit(k)
-            t = work.tile([P, 8, P64], F32, name="prod", tag="prod", bufs=8, align_bytes=64)
+            t = work.tile([P, 8, P64], F32, name="prod", tag="prod", bufs=6, align_bytes=64)
             if eng == "v":
                 nc.vector.tensor_tensor(out=t[:], in0=dms[k][:].rearrange("c (i w) -> c i w", i=8),
                                         in1=qt[:, ct, 8 * g:8 * g + 8].unsqueeze(2).to_broadcast([P, 8, P64]), op=MULT)
@@ -139,7 +141,7 @@ def tile_rpn_modulator_pb_v_kernel(tc, q, feats, po_w, po_b, grad_out, out_0, ou
             b, ct, octet, g = unit(k)
             if octet == 0 and (b == 0 or ct == 0):
                 if b == 0:
-                    daccs[b, ct] = psum.tile([P, P], F32, name="dacc0", tag="oacc%d" % ct, bufs=1)
+                    daccs[b, ct] = psum.tile([P, P], F32, name="dacc0", tag="dacc" if ct == 3 else "oacc%d" % ct, bufs=1)
                 else:
                     t = psum.tile([P, 4, P], F32, name="dacc", tag="dacc", bufs=1)
                     dfull[b] = t[:]
@@ -150,7 +152,7 @@ def tile_rpn_modulator_pb_v_kernel(tc, q, feats, po_w, po_b, grad_out, out_0, ou
                                  rhs=ident_f[:], is_transpose=True, start=(octet == 0 and h == 0), stop=(octet == 3 and h == 3))
 
         def fin_s(b):
-            dsums[b] = work.tile([P, 4, P], F32, name="dsum", tag="dsum", bufs=2, align_bytes=64)
+            dsums[b] = work.tile([P, 4, P], F32, name="dsum", tag="dsum", bufs=1, align_bytes=64)
             if b == 0:
                 for ct in range(4):
                     nc.scalar.copy(out=dsums[b][:, ct], in_=daccs[b, ct][:])
@@ -161,7 +163,7 @@ def tile_rpn_modulator_pb_v_kernel(tc, q, feats, po_w, po_b, grad_out, out_0, ou
         backs = {}
 
         def fin_t(b):
-            t = psum.tile([P, 4, P], F32, name="back", tag="x", bufs=3)
+            t = psum.tile([P, 4, P], F32, name="back", tag="x", bufs=4)
             for ct in range(4):
                 nc.tensor.transpose(t[:, ct, :], dsums[b][:, ct, :], ident_f[:])
             backs[b] = t
@@ -169,7 +171,7 @@ def tile_rpn_modulator_pb_v_kernel(tc, q, feats, po_w, po_b, grad_out, out_0, ou
         halves = {}
 
         def fin_h(b):
-            halves[b] = work.tile([P, 4, P], F32, name="half", tag="half", bufs=2, align_bytes=64)
+            halves[b] = work.tile([P, 4, P], F32, name="half", tag="half", bufs=1, align_bytes=64)
             nc.scalar.copy(out=halves[b][:], in_=backs[b][:])
 
         def fin_v(b):
@@ -193,7 +195,7 @@ def tile_rpn_modulator_pb_v_kernel(tc, q, feats, po_w, po_b, grad_out, out_0, ou
                 nc.scalar.copy(out=dst, in_=words[:, u])
 
         def b2(g, jh):
-            t = psum.tile([P, 2, 2, P], F32, name="tr", tag="x", bufs=3)
+            t = psum.tile([P, 2, 2, P], F32, name="tr", tag="x", bufs=4)
             for j2 in range(2):
                 for u in range(2):
                     pairs = raws[g][:, 2 * jh + j2].rearrange("q i w -> q (i w)").bitcast(F32)[:, u::2] if by_o(g) else rs[g][:, u, 2 * jh + j2, :]
@@ -202,7 +204,7 @@ def tile_rpn_modulator_pb_v_kernel(tc, q, feats, po_w, po_b, grad_out, out_0, ou
 
         def b3(g, jh):
             if jh == 0:
-                gbs[g] = work.tile([P, 4, P, 4], BF16, name="gb", tag="gb", bufs=3, align_bytes=64)
+                gbs[g] = work.tile([P, 4, P, 4], BF16, name="gb", tag="gb", bufs=2, align_bytes=64)
             dst = gbs[g][:, 2 * jh:2 * jh + 2].rearrange("t j q e -> t (j q e)").bitcast(F32).rearrange(
                 "t (j q u) -> t j q u", j=2, u=2)
             nc.scalar.copy(out=dst, in_=trs[g, jh][:].rearrange("t j u q -> t j q u"))
@@ -210,8 +212,8 @@ def tile_rpn_modulator_pb_v_kernel(tc, q, feats, po_w, po_b, grad_out, out_0, ou
         gbc, gbsc, mbc, mbsc, mbs = {}, {}, {}, {}, {}
 
         def b4(g):
-            gbc[g] = work.tile([P, C], U32, name="gbc", tag="gbc", bufs=3, align_bytes=64)
-            gbsc[g] = work.tile([P, C], U8, name="gbsc", tag="gbsc", bufs=3, align_bytes=64)
+            gbc[g] = work.tile([P, C], U32, name="gbc", tag="gbc", bufs=16, align_bytes=64)
+            gbsc[g] = work.tile([P, C], U8, name="gbsc", tag="gbsc", bufs=16, align_bytes=64)
             nc.vector.quantize_mx(out=gbc[g][:].bitcast(E5M2), scales=gbsc[g][:],
                                   in_=gbs[g][:].rearrange("t j q e -> t (j q e)"))
 
@@ -219,12 +221,12 @@ def tile_rpn_modulator_pb_v_kernel(tc, q, feats, po_w, po_b, grad_out, out_0, ou
             t = work.tile([P, C, 2, 2], BF16, name="mb", tag="mb", bufs=2, align_bytes=64)
             nc.vector.tensor_tensor(
                 out=t[:], in0=fbs[g // 4][:],
-                in1=q_all[:, g].bitcast(BF16).rearrange("p (c e) -> p c e", e=2).unsqueeze(2).to_broadcast([P, C, 2, 2]), op=MULT)
+                in1=qspread[g][:].bitcast(BF16).rearrange("p (c e) -> p c e", e=2).unsqueeze(2).to_broadcast([P, C, 2, 2]), op=MULT)
             mbs[g] = t
 
         def m3(g):
-            mbc[g] = work.tile([P, C], U32, name="mbc", tag="mbc", bufs=3, align_bytes=64)
-            mbsc[g] = work.tile([P, C], U8, name="mbsc", tag="mbsc", bufs=3, align_bytes=64)
+            mbc[g] = work.tile([P, C], U32, name="mbc", tag="mbc", bufs=16, align_bytes=64)
+            mbsc[g] = work.tile([P, C], U8, name="mbsc", tag="mbsc", bufs=16, align_bytes=64)
             nc.vector.quantize_mx(out=mbc[g][:].bitcast(E4M3), scales=mbsc[g][:],
                                   in_=mbs[g][:].rearrange("t c u e -> t (c u e)"))
 
@@ -238,7 +240,7 @@ def tile_rpn_modulator_pb_v_kernel(tc, q, feats, po_w, po_b, grad_out, out_0, ou
             freps[b] = t
 
         def f2(b, kh):
-            t = psum.tile([P, 2, 2, P], F32, name="ftr", tag="x", bufs=3)
+            t = psum.tile([P, 2, 2, P], F32, name="ftr", tag="x", bufs=4)
             for k2 in range(2):
                 for u in range(2):
                     nc.tensor.transpose(t[:, k2, u, :], freps[b][:, 2 * kh + k2, u].rearrange("r i h -> r (i h)"), ident_f[:])
@@ -246,7 +248,7 @@ def tile_rpn_modulator_pb_v_kernel(tc, q, feats, po_w, po_b, grad_out, out_0, ou
 
         def f3(b, kh):
             if kh == 0:
-                fbs[b] = work.tile([P, C, 2, 2], BF16, name="fb", tag="fb", bufs=3, align_bytes=64)
+                fbs[b] = work.tile([P, C, 2, 2], BF16, name="fb", tag="fb", bufs=2, align_bytes=64)
             dst = fbs[b][:, 2 * kh * P:(2 * kh + 2) * P].rearrange("t c u e -> t (c u e)").bitcast(F32).rearrange(
                 "t (k r u) -> t k r u", k=2, u=2)
             nc.scalar.copy(out=dst, in_=ftr[b, kh][:].rearrange("t k u r -> t k r u"))
@@ -256,7 +258,7 @@ def tile_rpn_modulator_pb_v_kernel(tc, q, feats, po_w, po_b, grad_out, out_0, ou
         def o(g, js):
             for j in js:
                 if g == 0:
-                    out_acc[j] = psum.tile([P, C], F32, name="oacc", tag="oacc%d" % j, bufs=1)
+                    out_acc[j] = psum.tile([P, C], F32, name="oacc", tag="dacc" if j == 3 else "oacc%d" % j, bufs=1)
                 cols = slice(j * P, (j + 1) * P)
                 nc.tensor.matmul_mx(out=out_acc[j][:], lhsT=gbc[g][:, cols].bitcast(E5M2), lhsT_scale=gbsc[g][:, cols],
                                     rhs=mbc[g][:].bitcast(E4M3), rhs_scale=mbsc[g][:],
@@ -264,7 +266,7 @@ def tile_rpn_modulator_pb_v_kernel(tc, q, feats, po_w, po_b, grad_out, out_0, ou
 
         def inter(g):
             for part in range(2):
-                a1(g, part, "s" if g == 0 and part == 0 else "v")
+                a1(g, part, "s" if False else "v")
 
         LAST = PASSES - 1
 
@@ -276,7 +278,7 @@ def tile_rpn_modulator_pb_v_kernel(tc, q, feats, po_w, po_b, grad_out, out_0, ou
             if g <= LAST:
                 a2(g)
 
-        qt_ps = psum.tile([P, 4, P], BF16, name="qt_ps", tag="x", bufs=3)
+        qt_ps = psum.tile([P, 4, P], BF16, name="qt_ps", tag="x", bufs=4)
         for ct in range(4):
             nc.tensor.transpose(qt_ps[:, ct, :], q_sort[:, ct, :], ident_b[:])
         qt = keep.tile([P, 4, P], F32, name="qt", align_bytes=64)
@@ -284,10 +286,10 @@ def tile_rpn_modulator_pb_v_kernel(tc, q, feats, po_w, po_b, grad_out, out_0, ou
         w_grp = keep.tile([P, 4, P, 4], BF16, name="w_grp", align_bytes=64)
         w_codes = keep.tile([P, C], U32, name="w_codes", align_bytes=64)
         w_scales = keep.tile([P, C], U8, name="w_scales", align_bytes=64)
+        nc.scalar.copy(out=w_grp[:], in_=w_raw[:].rearrange("q j (m k) -> q k m j", k=4))
         inter(0)
-        nc.vector.tensor_copy(out=w_grp[:], in_=w_raw[:].rearrange("q j (m k) -> q k m j", k=4))
-        a2(0)
         nc.vector.quantize_mx(out=w_codes[:].bitcast(E4M3), scales=w_scales[:], in_=w_grp[:].rearrange("q k m j -> q (k m j)"))
+        a2(0)
 
         def on_v(k):
             return False
@@ -303,10 +305,10 @@ def tile_rpn_modulator_pb_v_kernel(tc, q, feats, po_w, po_b, grad_out, out_0, ou
             j = s - BL
             D = s < PASSES
             a_new = early.get(s, (s + 4,) if s + 4 <= LAST else ())
-            if s + 5 + 2 <= LAST and s + 5 + 2 > 7:
-                load(s + 5 + 2)
-            if s + 2 <= LAST:
-                load_q(s + 2)
+            if s + 4 + 2 <= LAST and s + 4 + 2 > 7:
+                load(s + 4 + 2)
+            if 2 <= s - 1 <= LAST:
+                load_q(s - 1)
             pk = 4 * (s - 1)
             P0 = 1 <= s <= PASSES
             if P0:
@@ -328,7 +330,7 @@ def tile_rpn_modulator_pb_v_kernel(tc, q, feats, po_w, po_b, grad_out, out_0, ou
                 fin_t(s // 4 - 1)
                 fin_h(s // 4 - 1)
             if 0 <= j <= LAST:
-                b1(j, 0, "s" if False else "v")
+                b1(j, 0, "s" if j >= 15 else "v")
                 b1(j, 1, "v")
             for g in a_new:
                 prep(g)
@@ -346,14 +348,17 @@ def tile_rpn_modulator_pb_v_kernel(tc, q, feats, po_w, po_b, grad_out, out_0, ou
                 pd(4 * s + 2, "v" if on_v(4 * s + 2) else "s")
                 pd(4 * s + 3, "v" if on_v(4 * s + 3) else "s")
             if 0 <= j - 3 <= LAST:
-                o(j - 3, (2, 3))
+                o(j - 3, (2,))
+            if PASSES < s < STEPS - 1:
+                for g in range(5 * (s - PASSES - 1), min(5 * (s - PASSES), j - 2)):
+                    o(g, (3,))
             if 0 <= j - 2 <= LAST:
                 m3(j - 2)
             if 6 <= s and s % 4 == 2 and s <= PASSES + 2:
                 fin_v(s // 4 - 1)
-            if s == 1:
-                f1(0)
             if s == 2:
+                f1(0)
+            if s == 3:
                 f2(0, 0)
                 f3(0, 0)
                 f2(0, 1)
@@ -366,6 +371,8 @@ def tile_rpn_modulator_pb_v_kernel(tc, q, feats, po_w, po_b, grad_out, out_0, ou
             if s % 4 == 1 and 1 < s < 16:
                 f2(s // 4, 1)
                 f3(s // 4, 1)
+        for g in range(min(5 * (STEPS - 2 - PASSES), STEPS - BL - 4), PASSES):
+            o(g, (3,))
         res1 = keep.tile([P, 4, C], F32, name="res1", align_bytes=64)
         rows = out_1.rearrange("(q j) c -> q j c", j=4)
         for j in range(4):

from contextlib import ExitStack

import concourse.mybir as mybir
from concourse.masks import make_identity

B, I, C, P64 = 4, 32, 512, 64
PASSES = 16
FLOPS = 2 * 2 * 8192 * 512 * 512
BYTES = 2 * (4 * 32 * 512 + 4 * 512 * 64 + 512 * 512 + 4 * 32 * 512 * 64) + 4 * (4 * 512 * 64 + 512 * 512)

F32 = mybir.dt.float32
BF16 = mybir.dt.bfloat16
U32 = mybir.dt.uint32
U8 = mybir.dt.uint8
E4M3 = mybir.dt.float8_e4m3fn_x4
E5M2 = mybir.dt.float8_e5m2_x4
ADD = mybir.AluOpType.add
MULT = mybir.AluOpType.mult
COPY = mybir.ActivationFunctionType.Copy
AX = mybir.AxisListType.X
P = 128


def tile_rpn_modulator_pb_v_kernel(tc, q, feats, po_w, po_b, grad_out, out_0, out_1):
    nc = tc.nc
    with ExitStack() as ctx:
        keep = ctx.enter_context(tc.tile_pool(name="keep", bufs=1))
        work = ctx.enter_context(tc.tile_pool(name="work", bufs=2))
        psum = ctx.enter_context(tc.psum_pool(name="psum", bufs=1))
        ctx.enter_context(tc.manual_schedule())

        raws = {}

        def by_o(g):
            return False

        def load(g, pieces=1):
            if by_o(g):
                t = work.tile([P, 4, 8, P64], BF16, name="raw", tag="raw", bufs=8, align_bytes=64)
                b, i0 = g // 4, 8 * (g % 4)
                for j in range(4):
                    nc.sync.dma_start(
                        out=t[:, j], in_=grad_out[b, i0:i0 + 8].rearrange("i (q j) y x -> j q i (y x)", j=4)[j])
                raws[g] = t
                return
            t = work.tile([P, 8, 4, P64], BF16, name="raw", tag="raw", bufs=8, align_bytes=64)
            b, i0 = g // 4, 8 * (g % 4)
            n = 8 // pieces
            for k in range(pieces):
                nc.sync.dma_start(
                    out=t[:, k * n:(k + 1) * n].rearrange("q i j w -> q i (j w)"),
                    in_=grad_out[b, i0 + k * n:i0 + (k + 1) * n].rearrange("i (q j) y x -> q i (j y x)", j=4))
            raws[g] = t

        q_sb = keep.tile([P, C], BF16, name="q_sb", align_bytes=64)
        nc.sync.dma_start(out=q_sb[:], in_=q.rearrange("b i c -> (b i) c"))
        w_raw = keep.tile([P, 4, C], BF16, name="w_raw", align_bytes=64)
        nc.sync.dma_start(out=w_raw[:], in_=po_w.rearrange("(q j) c -> q j c", j=4))
        load(0, 2)
        load(1)
        load(2)
        load(3)
        load(4)

        ident_f = keep.tile([P, P], F32, name="ident_f", align_bytes=64)
        make_identity(nc, ident_f[:])
        ident_b = keep.tile([P, P], BF16, name="ident_b", align_bytes=64)
        make_identity(nc, ident_b[:])

        q_dup = keep.tile([P, C, 2], BF16, name="q_dup", align_bytes=64)
        nc.vector.tensor_copy(out=q_dup[:], in_=q_sb[:].unsqueeze(2).to_broadcast([P, C, 2]))
        q_sort = keep.tile([P, 4, P], BF16, name="q_sort", align_bytes=64)
        nc.vector.tensor_copy(out=q_sort[:], in_=q_sb[:].rearrange("p (m k) -> p k m", k=4))
        f_sb = keep.tile([P, 16, P64], BF16, name="f_sb", align_bytes=64)
        nc.sync.dma_start(out=out_1[0:P, :], in_=q_dup[:].rearrange("p c e -> p (c e)").bitcast(F32))
        qspread = {}

        def load_q(g):
            qspread[g] = work.tile([P, C], F32, name="qsp", tag="qsp", bufs=5, align_bytes=64)
            nc.sync.dma_start(out=qspread[g][:], in_=out_1[8 * g:8 * g + 8, :].unsqueeze(1).to_broadcast([8, 16, C]))

        load(5)
        load(6)
        load(7)
        nc.sync.dma_start(out=f_sb[:], in_=feats.rearrange("b (k r) y x -> r (b k) (y x)", r=P))
        load_q(0)
        load_q(1)

        gas, gacs, gass = {}, {}, {}

        def a1(g, half, eng):
            if half == 0:
                gas[g] = work.tile([P, 8, P64, 4], BF16, name="ga", tag="ga", bufs=2, align_bytes=64)
            sl = slice(4 * half, 4 * half + 4)
            if by_o(g):
                src = raws[g][:, :, sl].rearrange("q j i w -> q j (i w)")
                src = src.rearrange("q j (c k) -> q c j k", k=4)
                dst = gas[g][:, sl].rearrange("q i w j -> q (i w) j").rearrange("q (c k) j -> q c j k", k=4)
            else:
                src = raws[g][:, sl].rearrange("q i j (c k) -> q i c j k", k=4)
                dst = gas[g][:, sl].rearrange("q i (c k) j -> q i c j k", k=4)
            if eng == "v":
                nc.vector.tensor_copy(out=dst, in_=src)
            else:
                nc.scalar.copy(out=dst, in_=src)

        def a2(g):
            c = work.tile([P, C], U32, name="gac", tag="gac", bufs=8, align_bytes=64)
            s = work.tile([P, C], U8, name="gsc", tag="gsc", bufs=8, align_bytes=64)
            nc.vector.quantize_mx(out=c[:].bitcast(E5M2), scales=s[:], in_=gas[g][:].rearrange("q i w j -> q (i w j)"))
            gacs[g], gass[g] = c, s

        def unit(k):
            b = k // 16
            ct, octet = (k % 4, k // 4) if b == 0 else ((k // 4) % 4, k % 4)
            return b, ct, octet, 4 * b + octet

        dms, prods, daccs, dsums = {}, {}, {}, {}

        def dm(k):
            b, ct, octet, g = unit(k)
            t = psum.tile([P, C], F32, name="dm", tag="x", bufs=4)
            cols = slice(ct * P, (ct + 1) * P)
            nc.tensor.matmul_mx(out=t[:], lhsT=w_codes[:, cols].bitcast(E4M3), lhsT_scale=w_scales[:, cols],
                                rhs=gacs[g][:].bitcast(E5M2), rhs_scale=gass[g][:], start=True, stop=True)
            dms[k] = t

        def prod(k, eng):
            b, ct, octet, g = unit(k)
            t = work.tile([P, 8, P64], F32, name="prod", tag="prod", bufs=6, align_bytes=64)
            if eng == "v":
                nc.vector.tensor_tensor(out=t[:], in0=dms[k][:].rearrange("c (i w) -> c i w", i=8),
                                        in1=qt[:, ct, 8 * g:8 * g + 8].unsqueeze(2).to_broadcast([P, 8, P64]), op=MULT)
            else:
                for i in range(8):
                    nc.scalar.activation(out=t[:, i, :], in_=dms[k][:, i * P64:(i + 1) * P64], func=COPY,
                                         scale=qt[:, ct, 8 * g + i:8 * g + i + 1])
            prods[k] = t

        def acct(k):
            b, ct, octet, g = unit(k)
            if octet == 0 and (b == 0 or ct == 0):
                if b == 0:
                    daccs[b, ct] = psum.tile([P, P], F32, name="dacc0", tag="dacc" if ct == 3 else "oacc%d" % ct, bufs=1)
                else:
                    t = psum.tile([P, 4, P], F32, name="dacc", tag="dacc", bufs=1)
                    dfull[b] = t[:]
                    for j in range(4):
                        daccs[b, j] = t[:, j]
            for h in range(4):
                nc.tensor.matmul(daccs[b, ct][:], lhsT=prods[k][:, 2 * h:2 * h + 2].rearrange("c i w -> c (i w)"),
                                 rhs=ident_f[:], is_transpose=True, start=(octet == 0 and h == 0), stop=(octet == 3 and h == 3))

        def fin_s(b):
            dsums[b] = work.tile([P, 4, P], F32, name="dsum", tag="dsum", bufs=1, align_bytes=64)
            if b == 0:
                for ct in range(4):
                    nc.scalar.copy(out=dsums[b][:, ct], in_=daccs[b, ct][:])
            else:
                nc.scalar.copy(out=dsums[b][:], in_=dfull[b])

        dfull = {}
        backs = {}

        def fin_t(b):
            t = psum.tile([P, 4, P], F32, name="back", tag="x", bufs=4)
            for ct in range(4):
                nc.tensor.transpose(t[:, ct, :], dsums[b][:, ct, :], ident_f[:])
            backs[b] = t

        halves = {}

        def fin_h(b):
            halves[b] = work.tile([P, 4, P], F32, name="half", tag="half", bufs=1, align_bytes=64)
            nc.scalar.copy(out=halves[b][:], in_=backs[b][:])

        def fin_v(b):
            r = work.tile([P, 4, P64], F32, name="res0", tag="res0", bufs=2, align_bytes=64)
            nc.vector.tensor_tensor(out=r[:], in0=halves[b][:, :, 0:P64], in1=halves[b][:, :, P64:P], op=ADD)
            nc.sync.dma_start(out=out_0[b].rearrange("(m k) y x -> m (k y x)", k=4), in_=r[:].rearrange("m k w -> m (k w)"))

        rs, gbs, trs = {}, {}, {}

        def b1(g, u, eng):
            if by_o(g):
                return
            if u == 0:
                rs[g] = work.tile([P, 2, 4, P], F32, name="rw", tag="rw", bufs=2, align_bytes=64)
            words = raws[g][:].rearrange("q i j w -> q (i j w)").bitcast(F32).rearrange(
                "q (i j h u) -> q u j i h", i=8, j=4, u=2)
            dst = rs[g][:, u].rearrange("q j (i h) -> q j i h", i=8)
            if eng == "v":
                nc.vector.tensor_copy(out=dst, in_=words[:, u])
            else:
                nc.scalar.copy(out=dst, in_=words[:, u])

        def b2(g, jh):
            t = psum.tile([P, 2, 2, P], F32, name="tr", tag="x", bufs=4)
            for j2 in range(2):
                for u in range(2):
                    pairs = raws[g][:, 2 * jh + j2].rearrange("q i w -> q (i w)").bitcast(F32)[:, u::2] if by_o(g) else rs[g][:, u, 2 * jh + j2, :]
                    nc.tensor.transpose(t[:, j2, u, :], pairs, ident_f[:])
            trs[g, jh] = t

        def b3(g, jh):
            if jh == 0:
                gbs[g] = work.tile([P, 4, P, 4], BF16, name="gb", tag="gb", bufs=2, align_bytes=64)
            dst = gbs[g][:, 2 * jh:2 * jh + 2].rearrange("t j q e -> t (j q e)").bitcast(F32).rearrange(
                "t (j q u) -> t j q u", j=2, u=2)
            nc.scalar.copy(out=dst, in_=trs[g, jh][:].rearrange("t j u q -> t j q u"))

        gbc, gbsc, mbc, mbsc, mbs = {}, {}, {}, {}, {}

        def b4(g):
            gbc[g] = work.tile([P, C], U32, name="gbc", tag="gbc", bufs=16, align_bytes=64)
            gbsc[g] = work.tile([P, C], U8, name="gbsc", tag="gbsc", bufs=16, align_bytes=64)
            nc.vector.quantize_mx(out=gbc[g][:].bitcast(E5M2), scales=gbsc[g][:],
                                  in_=gbs[g][:].rearrange("t j q e -> t (j q e)"))

        def m2(g):
            t = work.tile([P, C, 2, 2], BF16, name="mb", tag="mb", bufs=2, align_bytes=64)
            nc.vector.tensor_tensor(
                out=t[:], in0=fbs[g // 4][:],
                in1=qspread[g][:].bitcast(BF16).rearrange("p (c e) -> p c e", e=2).unsqueeze(2).to_broadcast([P, C, 2, 2]), op=MULT)
            mbs[g] = t

        def m3(g):
            mbc[g] = work.tile([P, C], U32, name="mbc", tag="mbc", bufs=16, align_bytes=64)
            mbsc[g] = work.tile([P, C], U8, name="mbsc", tag="mbsc", bufs=16, align_bytes=64)
            nc.vector.quantize_mx(out=mbc[g][:].bitcast(E4M3), scales=mbsc[g][:],
                                  in_=mbs[g][:].rearrange("t c u e -> t (c u e)"))

        freps, ftr, fbs = {}, {}, {}

        def f1(b):
            t = work.tile([P, 4, 2, 8, 16], F32, name="frep", tag="frep", bufs=1, align_bytes=64)
            words = f_sb[:].rearrange("r k w -> r (k w)").bitcast(F32).rearrange("r (b k h u) -> r b u k h", b=4, k=4, u=2)
            for u in range(2):
                nc.vector.tensor_copy(out=t[:, :, u], in_=words[:, b, u].unsqueeze(2).to_broadcast([P, 4, 8, 16]))
            freps[b] = t

        def f2(b, kh):
            t = psum.tile([P, 2, 2, P], F32, name="ftr", tag="x", bufs=4)
            for k2 in range(2):
                for u in range(2):
                    nc.tensor.transpose(t[:, k2, u, :], freps[b][:, 2 * kh + k2, u].rearrange("r i h -> r (i h)"), ident_f[:])
            ftr[b, kh] = t

        def f3(b, kh):
            if kh == 0:
                fbs[b] = work.tile([P, C, 2, 2], BF16, name="fb", tag="fb", bufs=2, align_bytes=64)
            dst = fbs[b][:, 2 * kh * P:(2 * kh + 2) * P].rearrange("t c u e -> t (c u e)").bitcast(F32).rearrange(
                "t (k r u) -> t k r u", k=2, u=2)
            nc.scalar.copy(out=dst, in_=ftr[b, kh][:].rearrange("t k u r -> t k r u"))

        out_acc = {}

        def o(g, js):
            for j in js:
                if g == 0:
                    out_acc[j] = psum.tile([P, C], F32, name="oacc", tag="dacc" if j == 3 else "oacc%d" % j, bufs=1)
                cols = slice(j * P, (j + 1) * P)
                nc.tensor.matmul_mx(out=out_acc[j][:], lhsT=gbc[g][:, cols].bitcast(E5M2), lhsT_scale=gbsc[g][:, cols],
                                    rhs=mbc[g][:].bitcast(E4M3), rhs_scale=mbsc[g][:],
                                    start=(g == 0), stop=(g == PASSES - 1))

        def inter(g):
            for part in range(2):
                a1(g, part, "s" if False else "v")

        LAST = PASSES - 1

        def prep(g):
            if g <= LAST:
                inter(g)

        def quant(g):
            if g <= LAST:
                a2(g)

        qt_ps = psum.tile([P, 4, P], BF16, name="qt_ps", tag="x", bufs=4)
        for ct in range(4):
            nc.tensor.transpose(qt_ps[:, ct, :], q_sort[:, ct, :], ident_b[:])
        qt = keep.tile([P, 4, P], F32, name="qt", align_bytes=64)
        nc.vector.tensor_copy(out=qt[:], in_=qt_ps[:])
        w_grp = keep.tile([P, 4, P, 4], BF16, name="w_grp", align_bytes=64)
        w_codes = keep.tile([P, C], U32, name="w_codes", align_bytes=64)
        w_scales = keep.tile([P, C], U8, name="w_scales", align_bytes=64)
        nc.scalar.copy(out=w_grp[:], in_=w_raw[:].rearrange("q j (m k) -> q k m j", k=4))
        inter(0)
        nc.vector.quantize_mx(out=w_codes[:].bitcast(E4M3), scales=w_scales[:], in_=w_grp[:].rearrange("q k m j -> q (k m j)"))
        a2(0)

        def on_v(k):
            return False

        def pd(k, eng):
            dm(k)
            prod(k, eng)

        early = {0: (1, 2), 1: (3, 4), 2: (5, 6), 3: (7,)}
        BL = 2
        STEPS = PASSES + BL + 3
        for s in range(STEPS):
            j = s - BL
            D = s < PASSES
            a_new = early.get(s, (s + 4,) if s + 4 <= LAST else ())
            if s + 4 + 2 <= LAST and s + 4 + 2 > 7:
                load(s + 4 + 2)
            if 2 <= s - 1 <= LAST:
                load_q(s - 1)
            pk = 4 * (s - 1)
            P0 = 1 <= s <= PASSES
            if P0:
                acct(pk)
                acct(pk + 1)
            if 0 <= j - 1 <= LAST:
                b2(j - 1, 0)
                b2(j - 1, 1)
                b3(j - 1, 0)
                b3(j - 1, 1)
            if P0:
                acct(pk + 2)
                acct(pk + 3)
            if s == 4:
                fin_s(0)
            if s > 4 and s % 4 == 0 and s <= PASSES:
                fin_s(s // 4 - 1)
            if 5 <= s <= PASSES + 1 and s % 4 == 1:
                fin_t(s // 4 - 1)
                fin_h(s // 4 - 1)
            if 0 <= j <= LAST:
                b1(j, 0, "s" if j >= 15 else "v")
                b1(j, 1, "v")
            for g in a_new:
                prep(g)
            if D:
                pd(4 * s, "v" if on_v(4 * s) else "s")
                pd(4 * s + 1, "v" if on_v(4 * s + 1) else "s")
            if 0 <= j - 2 <= LAST:
                b4(j - 2)
                m2(j - 2)
            if 0 <= j - 3 <= LAST:
                o(j - 3, (0, 1))
            for g in a_new:
                quant(g)
            if D:
                pd(4 * s + 2, "v" if on_v(4 * s + 2) else "s")
                pd(4 * s + 3, "v" if on_v(4 * s + 3) else "s")
            if 0 <= j - 3 <= LAST:
                o(j - 3, (2,))
            if PASSES < s < STEPS - 1:
                for g in range(5 * (s - PASSES - 1), min(5 * (s - PASSES), j - 2)):
                    o(g, (3,))
            if 0 <= j - 2 <= LAST:
                m3(j - 2)
            if 6 <= s and s % 4 == 2 and s <= PASSES + 2:
                fin_v(s // 4 - 1)
            if s == 2:
                f1(0)
            if s == 3:
                f2(0, 0)
                f3(0, 0)
                f2(0, 1)
                f3(0, 1)
            if s % 4 == 3 and s < 12:
                f1(s // 4 + 1)
            if s % 4 == 0 and 0 < s < 16:
                f2(s // 4, 0)
                f3(s // 4, 0)
            if s % 4 == 1 and 1 < s < 16:
                f2(s // 4, 1)
                f3(s // 4, 1)
        for g in range(min(5 * (STEPS - 2 - PASSES), STEPS - BL - 4), PASSES):
            o(g, (3,))
        res1 = keep.tile([P, 4, C], F32, name="res1", align_bytes=64)
        rows = out_1.rearrange("(q j) c -> q j c", j=4)
        for j in range(4):
            if j % 2 == 1:
                nc.scalar.copy(out=res1[:, j], in_=out_acc[j][:])
            else:
                nc.vector.tensor_copy(out=res1[:, j], in_=out_acc[j][:])
            nc.sync.dma_start(out=rows[:, j], in_=res1[:, j])
